import numpy as np
import ml_dtypes

BF16 = ml_dtypes.bfloat16


def bf(x):
    return np.asarray(x, np.float32).astype(BF16)


def f32(x):
    return np.asarray(x, np.float32)


def f64(x):
    return np.asarray(x).astype(np.float64)


def striped(idx):
    return np.tile(idx.reshape(-1, 16).T, (8, 1))


D, M, S, RUN, K, E, N = 128, 128, 1024, 512, 4, 1024, 2048
CUTOFF = 5.0


def silu(v):
    return v / (1.0 + np.exp(-v))


def setup_inputs():
    return {
        "table": bf(np.random.standard_normal((D, S))),
        "w_src": bf(np.random.standard_normal((D, M)) / np.sqrt(D)),
        "w_dst": bf(np.random.standard_normal((D, M)) / np.sqrt(D)),
        "w_rbf": bf(np.random.standard_normal((D, M)) / np.sqrt(D)),
        "dist": f32(0.5 + 4.0 * np.random.random((1, E))),
        "w0": f32(3.0 * np.random.standard_normal((D, 1))),
        "b0": f32(0.5 * np.random.standard_normal((D, 1))),
        "b": f32(0.2 * np.random.standard_normal((M, 1))),
        "w1": f32(3.0 * np.random.standard_normal((M, 1))),
        "offs": striped(np.concatenate([np.random.permutation(S)[:RUN] for _ in range(K)])),
    }


def reference(table, w_src, w_dst, w_rbf, dist, w0, b0, b, w1, offs):
    idx = offs[:16].T.reshape(-1)
    t = f64(table)
    dd = f64(dist)
    rbf = np.sqrt(2.0 / CUTOFF) * np.sin(dd * (np.pi / CUTOFF)) / dd
    rbf0 = silu(f64(w0) * rbf + f64(b0))
    pre = f64(w_src).T @ t[:, idx[:E]] + f64(w_dst).T @ t[:, idx[E:]] + f64(w_rbf).T @ rbf0 + f64(b)
    return f64(w1) * rbf * silu(pre)

@@ -1,0 +1,71 @@
+import math
+
+import concourse.mybir as mybir
+
+FEATURES = 128
+NODES = 1024
+EDGES = 1024
+PIECE = 512
+CUTOFF = 5.0
+FLOPS = 2 * 3 * FEATURES * FEATURES * EDGES
+
+BF16, F32, U16 = mybir.dt.bfloat16, mybir.dt.float32, mybir.dt.uint16
+ACT = mybir.ActivationFunctionType
+MULT = mybir.AluOpType.mult
+
+
+def tile_edgefeatureinit_kernel(tc, table, w_src, w_dst, w_rbf, dist, w0, b0, b, w1, offs, out):
+    nc = tc.nc
+    with (
+        tc.tile_pool(name="held", bufs=1) as held,
+        tc.tile_pool(name="work", bufs=2) as work,
+        tc.psum_pool(name="psum", bufs=2) as psum,
+    ):
+        lengths = held.tile([FEATURES, EDGES], F32, name="lengths")
+        nc.scalar.dma_start(lengths[:], dist.rearrange("o e -> (o e)").partition_broadcast(FEATURES))
+
+        offsets = held.tile([FEATURES, 2 * EDGES // 16], U16, name="offsets")
+        nc.sync.dma_start(offsets[:], offs)
+        nodes = held.tile([FEATURES, NODES], BF16, name="nodes")
+        nc.sync.dma_start(nodes[:], table)
+        src_weights = held.tile([FEATURES, FEATURES], BF16, name="src_weights")
+        nc.sync.dma_start(src_weights[:], w_src)
+        dst_weights = held.tile([FEATURES, FEATURES], BF16, name="dst_weights")
+        nc.sync.dma_start(dst_weights[:], w_dst)
+        rbf_weights = held.tile([FEATURES, FEATURES], BF16, name="rbf_weights")
+        nc.sync.dma_start(rbf_weights[:], w_rbf)
+
+        w0_col = held.tile([FEATURES, 1], F32, name="w0_col")
+        nc.gpsimd.dma_start(w0_col[:], w0)
+        b0_col = held.tile([FEATURES, 1], F32, name="b0_col")
+        nc.gpsimd.dma_start(b0_col[:], b0)
+        b_col = held.tile([FEATURES, 1], F32, name="b_col")
+        nc.gpsimd.dma_start(b_col[:], b)
+        w1_col = held.tile([FEATURES, 1], F32, name="w1_col")
+        nc.gpsimd.dma_start(w1_col[:], w1)
+
+        sine = held.tile([FEATURES, EDGES], F32, name="sine")
+        nc.scalar.activation(sine[:], lengths[:], ACT.Sin, scale=math.pi / CUTOFF)
+
+        for piece in range(EDGES // PIECE):
+            edges = slice(piece * PIECE, (piece + 1) * PIECE)
+            src_list = offsets[:, piece * (PIECE // 16) : (piece + 1) * (PIECE // 16)]
+            dst_list = offsets[:, (EDGES + piece * PIECE) // 16 : (EDGES + (piece + 1) * PIECE) // 16]
+
+            pre = psum.tile([FEATURES, PIECE], F32, name="pre")
+            nc.tensor.matmul(pre[:], src_weights[:], nodes[:].indirect(src_list), start=True, stop=False)
+            nc.tensor.matmul(pre[:], dst_weights[:], nodes[:].indirect(dst_list), start=False, stop=False)
+
+            inverse = work.tile([FEATURES, PIECE], F32, name="inverse")
+            nc.vector.reciprocal(inverse[:], lengths[:, edges])
+            rbf = work.tile([FEATURES, PIECE], F32, name="rbf")
+            nc.vector.scalar_tensor_tensor(rbf[:], sine[:, edges], math.sqrt(2.0 / CUTOFF), inverse[:], MULT, MULT)
+            rbf0 = work.tile([FEATURES, PIECE], BF16, name="rbf0")
+            nc.scalar.activation(rbf0[:], rbf[:], ACT.Silu, bias=b0_col[:], scale=w0_col[:])
+            nc.tensor.matmul(pre[:], rbf_weights[:], rbf0[:], start=False, stop=True)
+
+            gated = work.tile([FEATURES, PIECE], F32, name="gated")
+            nc.scalar.activation(gated[:], pre[:], ACT.Silu, bias=b_col[:])
+            result = work.tile([FEATURES, PIECE], F32, name="result")
+            nc.vector.scalar_tensor_tensor(result[:], gated[:], w1_col[:], rbf[:], MULT, MULT)
+            nc.sync.dma_start(out[:, edges], result[:])

@@ -1,17 +1,20 @@
 import math
 
 import concourse.mybir as mybir
+from concourse.masks import make_identity
 
 FEATURES = 128
 NODES = 1024
 EDGES = 1024
 PIECE = 512
+ROWS = 16
+RUN = EDGES // ROWS
 CUTOFF = 5.0
 FLOPS = 2 * 3 * FEATURES * FEATURES * EDGES
 
-BF16, F32, U16 = mybir.dt.bfloat16, mybir.dt.float32, mybir.dt.uint16
+BF16, F32, I32, U16 = mybir.dt.bfloat16, mybir.dt.float32, mybir.dt.int32, mybir.dt.uint16
 ACT = mybir.ActivationFunctionType
-MULT = mybir.AluOpType.mult
+ALU = mybir.AluOpType
 
 
 def tile_edgefeatureinit_kernel(tc, table, w_src, w_dst, w_rbf, dist, w0, b0, b, w1, offs, out):
@@ -19,10 +22,10 @@ def tile_edgefeatureinit_kernel(tc, table, w_src, w_dst, w_rbf, dist, w0, b0, b,
     with (
         tc.tile_pool(name="held", bufs=1) as held,
         tc.tile_pool(name="work", bufs=2) as work,
-        tc.psum_pool(name="psum", bufs=2) as psum,
+        tc.psum_pool(name="psum", bufs=1) as psum,
     ):
-        lengths = held.tile([FEATURES, EDGES], F32, name="lengths")
-        nc.scalar.dma_start(lengths[:], dist.rearrange("o e -> (o e)").partition_broadcast(FEATURES))
+        lengths = held.tile([ROWS, RUN], F32, name="lengths")
+        nc.scalar.dma_start(lengths[:], dist.rearrange("o (r c) -> (o r) c", r=ROWS))
 
         offsets = held.tile([FEATURES, 2 * EDGES // 16], U16, name="offsets")
         nc.sync.dma_start(offsets[:], offs)
@@ -32,40 +35,58 @@ def tile_edgefeatureinit_kernel(tc, table, w_src, w_dst, w_rbf, dist, w0, b0, b,
         nc.sync.dma_start(src_weights[:], w_src)
         dst_weights = held.tile([FEATURES, FEATURES], BF16, name="dst_weights")
         nc.sync.dma_start(dst_weights[:], w_dst)
-        rbf_weights = held.tile([FEATURES, FEATURES], BF16, name="rbf_weights")
-        nc.sync.dma_start(rbf_weights[:], w_rbf)
 
         w0_col = held.tile([FEATURES, 1], F32, name="w0_col")
-        nc.gpsimd.dma_start(w0_col[:], w0)
+        nc.scalar.dma_start(w0_col[:], w0)
         b0_col = held.tile([FEATURES, 1], F32, name="b0_col")
-        nc.gpsimd.dma_start(b0_col[:], b0)
+        nc.scalar.dma_start(b0_col[:], b0)
+        rbf_weights = held.tile([FEATURES, FEATURES], BF16, name="rbf_weights")
+        nc.scalar.dma_start(rbf_weights[:], w_rbf)
         b_col = held.tile([FEATURES, 1], F32, name="b_col")
-        nc.gpsimd.dma_start(b_col[:], b)
+        nc.scalar.dma_start(b_col[:], b)
         w1_col = held.tile([FEATURES, 1], F32, name="w1_col")
-        nc.gpsimd.dma_start(w1_col[:], w1)
+        nc.scalar.dma_start(w1_col[:], w1)
 
-        sine = held.tile([FEATURES, EDGES], F32, name="sine")
-        nc.scalar.activation(sine[:], lengths[:], ACT.Sin, scale=math.pi / CUTOFF)
+        identity = held.tile([FEATURES, FEATURES], F32, name="identity")
+        make_identity(nc, identity[:])
+        rbf_rows = held.tile([FEATURES, RUN], F32, name="rbf_rows")
+        nc.vector.memset(rbf_rows[:], 0.0)
+
+        turns = held.tile([ROWS, RUN], I32, name="turns")
+        nc.vector.tensor_scalar(turns[:], lengths[:], 0.5 / CUTOFF, None, ALU.mult)
+        part = held.tile([ROWS, RUN], F32, name="part")
+        nc.vector.scalar_tensor_tensor(part[:], lengths[:], 0.5 / CUTOFF, turns[:], ALU.mult, ALU.subtract)
+        minus_t = held.tile([ROWS, RUN], F32, name="minus_t")
+        nc.vector.scalar_tensor_tensor(minus_t[:], part[:], 0.5, part[:], ALU.is_gt, ALU.subtract)
+        sine = held.tile([ROWS, RUN], F32, name="sine")
+        nc.scalar.activation(sine[:], minus_t[:], ACT.Sin, scale=-2.0 * math.pi)
+
+        inverse = held.tile([ROWS, RUN], F32, name="inverse")
+        nc.vector.reciprocal(inverse[:], lengths[:])
+        nc.vector.scalar_tensor_tensor(
+            rbf_rows[:ROWS, :], sine[:], math.sqrt(2.0 / CUTOFF), inverse[:], ALU.mult, ALU.mult
+        )
+
+        rbf = [psum.tile([FEATURES, PIECE], F32, name=f"rbf{piece}") for piece in range(EDGES // PIECE)]
+        for row in range(ROWS):
+            piece, first = divmod(row * RUN, PIECE)
+            pick_row = identity[:, row : row + 1].to_broadcast([FEATURES, FEATURES])
+            nc.tensor.matmul(rbf[piece][:, first : first + RUN], pick_row, rbf_rows[:], start=True, stop=True)
 
         for piece in range(EDGES // PIECE):
             edges = slice(piece * PIECE, (piece + 1) * PIECE)
             src_list = offsets[:, piece * (PIECE // 16) : (piece + 1) * (PIECE // 16)]
             dst_list = offsets[:, (EDGES + piece * PIECE) // 16 : (EDGES + (piece + 1) * PIECE) // 16]
 
-            pre = psum.tile([FEATURES, PIECE], F32, name="pre")
+            pre = psum.tile([FEATURES, PIECE], F32, name=f"pre{piece}")
             nc.tensor.matmul(pre[:], src_weights[:], nodes[:].indirect(src_list), start=True, stop=False)
             nc.tensor.matmul(pre[:], dst_weights[:], nodes[:].indirect(dst_list), start=False, stop=False)
-
-            inverse = work.tile([FEATURES, PIECE], F32, name="inverse")
-            nc.vector.reciprocal(inverse[:], lengths[:, edges])
-            rbf = work.tile([FEATURES, PIECE], F32, name="rbf")
-            nc.vector.scalar_tensor_tensor(rbf[:], sine[:, edges], math.sqrt(2.0 / CUTOFF), inverse[:], MULT, MULT)
             rbf0 = work.tile([FEATURES, PIECE], BF16, name="rbf0")
-            nc.scalar.activation(rbf0[:], rbf[:], ACT.Silu, bias=b0_col[:], scale=w0_col[:])
+            nc.scalar.activation(rbf0[:], rbf[piece][:], ACT.Silu, bias=b0_col[:], scale=w0_col[:])
             nc.tensor.matmul(pre[:], rbf_weights[:], rbf0[:], start=False, stop=True)
 
             gated = work.tile([FEATURES, PIECE], F32, name="gated")
             nc.scalar.activation(gated[:], pre[:], ACT.Silu, bias=b_col[:])
             result = work.tile([FEATURES, PIECE], F32, name="result")
-            nc.vector.scalar_tensor_tensor(result[:], gated[:], w1_col[:], rbf[:], MULT, MULT)
+            nc.vector.scalar_tensor_tensor(result[:], gated[:], w1_col[:], rbf[piece][:], ALU.mult, ALU.mult)
             nc.sync.dma_start(out[:, edges], result[:])

@@ -25,7 +25,7 @@ def tile_edgefeatureinit_kernel(tc, table, w_src, w_dst, w_rbf, dist, w0, b0, b,
         tc.psum_pool(name="psum", bufs=1) as psum,
     ):
         lengths = held.tile([ROWS, RUN], F32, name="lengths")
-        nc.scalar.dma_start(lengths[:], dist.rearrange("o (r c) -> (o r) c", r=ROWS))
+        nc.sync.dma_start(lengths[:], dist.rearrange("o (r c) -> (o r) c", r=ROWS))
 
         offsets = held.tile([FEATURES, 2 * EDGES // 16], U16, name="offsets")
         nc.sync.dma_start(offsets[:], offs)
@@ -36,16 +36,21 @@ def tile_edgefeatureinit_kernel(tc, table, w_src, w_dst, w_rbf, dist, w0, b0, b,
         dst_weights = held.tile([FEATURES, FEATURES], BF16, name="dst_weights")
         nc.sync.dma_start(dst_weights[:], w_dst)
 
+        rbf_weights = held.tile([FEATURES, FEATURES], BF16, name="rbf_weights")
+        nc.sync.dma_start(rbf_weights[:], w_rbf)
+
         w0_col = held.tile([FEATURES, 1], F32, name="w0_col")
         nc.scalar.dma_start(w0_col[:], w0)
         b0_col = held.tile([FEATURES, 1], F32, name="b0_col")
         nc.scalar.dma_start(b0_col[:], b0)
-        rbf_weights = held.tile([FEATURES, FEATURES], BF16, name="rbf_weights")
-        nc.scalar.dma_start(rbf_weights[:], w_rbf)
         b_col = held.tile([FEATURES, 1], F32, name="b_col")
-        nc.scalar.dma_start(b_col[:], b)
+        nc.sync.dma_start(b_col[:], b)
         w1_col = held.tile([FEATURES, 1], F32, name="w1_col")
-        nc.scalar.dma_start(w1_col[:], w1)
+        nc.sync.dma_start(w1_col[:], w1)
+
+        scratch = held.tile([FEATURES, 1], F32, name="scratch")
+        nc.vector.memset(scratch[:], 0.0)
+        nc.scalar.activation(scratch[:], scratch[:], ACT.Sin)
 
         identity = held.tile([FEATURES, FEATURES], F32, name="identity")
         make_identity(nc, identity[:])

@@ -7,8 +7,7 @@ FEATURES = 128
 NODES = 1024
 EDGES = 1024
 PIECE = 512
-ROWS = 16
-RUN = EDGES // ROWS
+RUN = EDGES // FEATURES
 CUTOFF = 5.0
 FLOPS = 2 * 3 * FEATURES * FEATURES * EDGES
 
@@ -24,25 +23,22 @@ def tile_edgefeatureinit_kernel(tc, table, w_src, w_dst, w_rbf, dist, w0, b0, b,
         tc.tile_pool(name="work", bufs=2) as work,
         tc.psum_pool(name="psum", bufs=1) as psum,
     ):
-        lengths = held.tile([ROWS, RUN], F32, name="lengths")
-        nc.sync.dma_start(lengths[:], dist.rearrange("o (r c) -> (o r) c", r=ROWS))
-
+        lengths = held.tile([FEATURES, RUN], F32, name="lengths")
+        nc.sync.dma_start(lengths[:], dist.rearrange("o (k c) -> (o k) c", c=RUN))
+        nodes = held.tile([FEATURES, NODES], BF16, name="nodes")
+        nc.scalar.dma_start(nodes[:], table)
         offsets = held.tile([FEATURES, 2 * EDGES // 16], U16, name="offsets")
         nc.sync.dma_start(offsets[:], offs)
-        nodes = held.tile([FEATURES, NODES], BF16, name="nodes")
-        nc.sync.dma_start(nodes[:], table)
         src_weights = held.tile([FEATURES, FEATURES], BF16, name="src_weights")
         nc.sync.dma_start(src_weights[:], w_src)
         dst_weights = held.tile([FEATURES, FEATURES], BF16, name="dst_weights")
         nc.sync.dma_start(dst_weights[:], w_dst)
-
-        rbf_weights = held.tile([FEATURES, FEATURES], BF16, name="rbf_weights")
-        nc.sync.dma_start(rbf_weights[:], w_rbf)
-
         w0_col = held.tile([FEATURES, 1], F32, name="w0_col")
         nc.scalar.dma_start(w0_col[:], w0)
         b0_col = held.tile([FEATURES, 1], F32, name="b0_col")
         nc.scalar.dma_start(b0_col[:], b0)
+        rbf_weights = held.tile([FEATURES, FEATURES], BF16, name="rbf_weights")
+        nc.sync.dma_start(rbf_weights[:], w_rbf)
         b_col = held.tile([FEATURES, 1], F32, name="b_col")
         nc.sync.dma_start(b_col[:], b)
         w1_col = held.tile([FEATURES, 1], F32, name="w1_col")
@@ -54,44 +50,48 @@ def tile_edgefeatureinit_kernel(tc, table, w_src, w_dst, w_rbf, dist, w0, b0, b,
 
         identity = held.tile([FEATURES, FEATURES], F32, name="identity")
         make_identity(nc, identity[:])
-        rbf_rows = held.tile([FEATURES, RUN], F32, name="rbf_rows")
-        nc.vector.memset(rbf_rows[:], 0.0)
+        ones = held.tile([FEATURES, FEATURES], F32, name="ones")
+        nc.vector.memset(ones[:], 1.0)
 
-        turns = held.tile([ROWS, RUN], I32, name="turns")
+        turns = held.tile([FEATURES, RUN], I32, name="turns")
         nc.vector.tensor_scalar(turns[:], lengths[:], 0.5 / CUTOFF, None, ALU.mult)
-        part = held.tile([ROWS, RUN], F32, name="part")
+        part = held.tile([FEATURES, RUN], F32, name="part")
         nc.vector.scalar_tensor_tensor(part[:], lengths[:], 0.5 / CUTOFF, turns[:], ALU.mult, ALU.subtract)
-        minus_t = held.tile([ROWS, RUN], F32, name="minus_t")
+        minus_t = held.tile([FEATURES, RUN], F32, name="minus_t")
         nc.vector.scalar_tensor_tensor(minus_t[:], part[:], 0.5, part[:], ALU.is_gt, ALU.subtract)
-        sine = held.tile([ROWS, RUN], F32, name="sine")
+        sine = held.tile([FEATURES, RUN], F32, name="sine")
         nc.scalar.activation(sine[:], minus_t[:], ACT.Sin, scale=-2.0 * math.pi)
 
-        inverse = held.tile([ROWS, RUN], F32, name="inverse")
+        inverse = held.tile([FEATURES, RUN], F32, name="inverse")
         nc.vector.reciprocal(inverse[:], lengths[:])
-        nc.vector.scalar_tensor_tensor(
-            rbf_rows[:ROWS, :], sine[:], math.sqrt(2.0 / CUTOFF), inverse[:], ALU.mult, ALU.mult
-        )
-
-        rbf = [psum.tile([FEATURES, PIECE], F32, name=f"rbf{piece}") for piece in range(EDGES // PIECE)]
-        for row in range(ROWS):
-            piece, first = divmod(row * RUN, PIECE)
-            pick_row = identity[:, row : row + 1].to_broadcast([FEATURES, FEATURES])
-            nc.tensor.matmul(rbf[piece][:, first : first + RUN], pick_row, rbf_rows[:], start=True, stop=True)
+        rbf_small = held.tile([FEATURES, RUN], F32, name="rbf_small")
+        nc.vector.scalar_tensor_tensor(rbf_small[:], sine[:], math.sqrt(2.0 / CUTOFF), inverse[:], ALU.mult, ALU.mult)
 
         for piece in range(EDGES // PIECE):
             edges = slice(piece * PIECE, (piece + 1) * PIECE)
             src_list = offsets[:, piece * (PIECE // 16) : (piece + 1) * (PIECE // 16)]
             dst_list = offsets[:, (EDGES + piece * PIECE) // 16 : (EDGES + (piece + 1) * PIECE) // 16]
+            owners = slice(piece * (PIECE // RUN), (piece + 1) * (PIECE // RUN))
+
+            spread = work.tile([FEATURES, PIECE // RUN, RUN], F32, name="spread")
+            nc.vector.tensor_tensor(
+                spread[:],
+                identity[:, owners].unsqueeze(2).to_broadcast([FEATURES, PIECE // RUN, RUN]),
+                rbf_small[:].unsqueeze(1).to_broadcast([FEATURES, PIECE // RUN, RUN]),
+                ALU.mult,
+            )
+            rbf = psum.tile([FEATURES, PIECE], F32, name=f"rbf{piece}")
+            nc.tensor.matmul(rbf[:], ones[:], spread[:].rearrange("k q c -> k (q c)"), start=True, stop=True)
 
             pre = psum.tile([FEATURES, PIECE], F32, name=f"pre{piece}")
             nc.tensor.matmul(pre[:], src_weights[:], nodes[:].indirect(src_list), start=True, stop=False)
             nc.tensor.matmul(pre[:], dst_weights[:], nodes[:].indirect(dst_list), start=False, stop=False)
             rbf0 = work.tile([FEATURES, PIECE], BF16, name="rbf0")
-            nc.scalar.activation(rbf0[:], rbf[piece][:], ACT.Silu, bias=b0_col[:], scale=w0_col[:])
+            nc.scalar.activation(rbf0[:], rbf[:], ACT.Silu, bias=b0_col[:], scale=w0_col[:])
             nc.tensor.matmul(pre[:], rbf_weights[:], rbf0[:], start=False, stop=True)
 
             gated = work.tile([FEATURES, PIECE], F32, name="gated")
             nc.scalar.activation(gated[:], pre[:], ACT.Silu, bias=b_col[:])
             result = work.tile([FEATURES, PIECE], F32, name="result")
-            nc.vector.scalar_tensor_tensor(result[:], gated[:], w1_col[:], rbf[piece][:], ALU.mult, ALU.mult)
+            nc.vector.scalar_tensor_tensor(result[:], gated[:], w1_col[:], rbf[:], ALU.mult, ALU.mult)
             nc.sync.dma_start(out[:, edges], result[:])

@@ -8,6 +8,7 @@ NODES = 1024
 EDGES = 1024
 PIECE = 512
 RUN = EDGES // FEATURES
+WARM_UP = 6
 CUTOFF = 5.0
 FLOPS = 2 * 3 * FEATURES * FEATURES * EDGES
 
@@ -47,6 +48,12 @@ def tile_edgefeatureinit_kernel(tc, table, w_src, w_dst, w_rbf, dist, w0, b0, b,
         scratch = held.tile([FEATURES, 1], F32, name="scratch")
         nc.vector.memset(scratch[:], 0.0)
         nc.scalar.activation(scratch[:], scratch[:], ACT.Sin)
+
+        zeros = held.tile([FEATURES, PIECE], BF16, name="zeros")
+        nc.vector.memset(zeros[:], 0.0)
+        unused = psum.tile([FEATURES, PIECE], F32, name="unused")
+        for turn in range(WARM_UP):
+            nc.tensor.matmul(unused[:], zeros[:, :FEATURES], zeros[:], start=True, stop=True)
 
         identity = held.tile([FEATURES, FEATURES], F32, name="identity")
         make_identity(nc, identity[:])

@@ -1,14 +1,13 @@
 import math
 
 import concourse.mybir as mybir
-from concourse.masks import make_identity
 
 FEATURES = 128
 NODES = 1024
 EDGES = 1024
 PIECE = 512
-RUN = EDGES // FEATURES
-WARM_UP = 6
+BLOCK = 32
+RUNS = EDGES // BLOCK
 CUTOFF = 5.0
 FLOPS = 2 * 3 * FEATURES * FEATURES * EDGES
 
@@ -24,14 +23,16 @@ def tile_edgefeatureinit_kernel(tc, table, w_src, w_dst, w_rbf, dist, w0, b0, b,
         tc.tile_pool(name="work", bufs=2) as work,
         tc.psum_pool(name="psum", bufs=1) as psum,
     ):
-        lengths = held.tile([FEATURES, RUN], F32, name="lengths")
-        nc.sync.dma_start(lengths[:], dist.rearrange("o (k c) -> (o k) c", c=RUN))
-        nodes = held.tile([FEATURES, NODES], BF16, name="nodes")
-        nc.scalar.dma_start(nodes[:], table)
         offsets = held.tile([FEATURES, 2 * EDGES // 16], U16, name="offsets")
         nc.sync.dma_start(offsets[:], offs)
+        nodes = held.tile([FEATURES, NODES], BF16, name="nodes")
+        nc.scalar.dma_start(nodes[:], table)
         src_weights = held.tile([FEATURES, FEATURES], BF16, name="src_weights")
         nc.sync.dma_start(src_weights[:], w_src)
+        runs = held.tile([FEATURES, BLOCK], F32, name="runs", align_bytes=64)
+        for group in range(FEATURES // BLOCK):
+            queue = nc.sync if group % 2 == 0 else nc.scalar
+            queue.dma_start(runs[group * BLOCK : (group + 1) * BLOCK, :], dist.rearrange("o (k i) -> (o k) i", i=BLOCK))
         dst_weights = held.tile([FEATURES, FEATURES], BF16, name="dst_weights")
         nc.sync.dma_start(dst_weights[:], w_dst)
         w0_col = held.tile([FEATURES, 1], F32, name="w0_col")
@@ -49,46 +50,38 @@ def tile_edgefeatureinit_kernel(tc, table, w_src, w_dst, w_rbf, dist, w0, b0, b,
         nc.vector.memset(scratch[:], 0.0)
         nc.scalar.activation(scratch[:], scratch[:], ACT.Sin)
 
-        zeros = held.tile([FEATURES, PIECE], BF16, name="zeros")
-        nc.vector.memset(zeros[:], 0.0)
-        unused = psum.tile([FEATURES, PIECE], F32, name="unused")
-        for turn in range(WARM_UP):
-            nc.tensor.matmul(unused[:], zeros[:, :FEATURES], zeros[:], start=True, stop=True)
+        lengths = held.tile([FEATURES, RUNS], F32, name="lengths", align_bytes=64)
+        nc.vector.transpose(lengths[:], runs[:])
 
-        identity = held.tile([FEATURES, FEATURES], F32, name="identity")
-        make_identity(nc, identity[:])
-        ones = held.tile([FEATURES, FEATURES], F32, name="ones")
-        nc.vector.memset(ones[:], 1.0)
-
-        turns = held.tile([FEATURES, RUN], I32, name="turns")
+        turns = held.tile([FEATURES, RUNS], I32, name="turns")
         nc.vector.tensor_scalar(turns[:], lengths[:], 0.5 / CUTOFF, None, ALU.mult)
-        part = held.tile([FEATURES, RUN], F32, name="part")
+        part = held.tile([FEATURES, RUNS], F32, name="part")
         nc.vector.scalar_tensor_tensor(part[:], lengths[:], 0.5 / CUTOFF, turns[:], ALU.mult, ALU.subtract)
-        minus_t = held.tile([FEATURES, RUN], F32, name="minus_t")
+        minus_t = held.tile([FEATURES, RUNS], F32, name="minus_t")
         nc.vector.scalar_tensor_tensor(minus_t[:], part[:], 0.5, part[:], ALU.is_gt, ALU.subtract)
-        sine = held.tile([FEATURES, RUN], F32, name="sine")
+        sine = held.tile([FEATURES, RUNS], F32, name="sine")
         nc.scalar.activation(sine[:], minus_t[:], ACT.Sin, scale=-2.0 * math.pi)
-
-        inverse = held.tile([FEATURES, RUN], F32, name="inverse")
+        inverse = held.tile([FEATURES, RUNS], F32, name="inverse")
         nc.vector.reciprocal(inverse[:], lengths[:])
-        rbf_small = held.tile([FEATURES, RUN], F32, name="rbf_small")
-        nc.vector.scalar_tensor_tensor(rbf_small[:], sine[:], math.sqrt(2.0 / CUTOFF), inverse[:], ALU.mult, ALU.mult)
 
         for piece in range(EDGES // PIECE):
             edges = slice(piece * PIECE, (piece + 1) * PIECE)
             src_list = offsets[:, piece * (PIECE // 16) : (piece + 1) * (PIECE // 16)]
             dst_list = offsets[:, (EDGES + piece * PIECE) // 16 : (EDGES + (piece + 1) * PIECE) // 16]
-            owners = slice(piece * (PIECE // RUN), (piece + 1) * (PIECE // RUN))
+            piece_runs = slice(piece * (PIECE // BLOCK), (piece + 1) * (PIECE // BLOCK))
+            wide = [FEATURES, PIECE // BLOCK, BLOCK]
 
-            spread = work.tile([FEATURES, PIECE // RUN, RUN], F32, name="spread")
-            nc.vector.tensor_tensor(
-                spread[:],
-                identity[:, owners].unsqueeze(2).to_broadcast([FEATURES, PIECE // RUN, RUN]),
-                rbf_small[:].unsqueeze(1).to_broadcast([FEATURES, PIECE // RUN, RUN]),
+            repeated = work.tile(wide, F32, name="repeated", align_bytes=64)
+            nc.vector.scalar_tensor_tensor(
+                repeated[:],
+                sine[:, piece_runs].unsqueeze(2).to_broadcast(wide),
+                math.sqrt(2.0 / CUTOFF),
+                inverse[:, piece_runs].unsqueeze(2).to_broadcast(wide),
+                ALU.mult,
                 ALU.mult,
             )
-            rbf = psum.tile([FEATURES, PIECE], F32, name=f"rbf{piece}")
-            nc.tensor.matmul(rbf[:], ones[:], spread[:].rearrange("k q c -> k (q c)"), start=True, stop=True)
+            rbf = work.tile([FEATURES, PIECE], F32, name="rbf", align_bytes=64)
+            nc.vector.transpose(rbf[:], repeated[:].rearrange("p k i -> p (k i)"))
 
             pre = psum.tile([FEATURES, PIECE], F32, name=f"pre{piece}")
             nc.tensor.matmul(pre[:], src_weights[:], nodes[:].indirect(src_list), start=True, stop=False)

@@ -5,7 +5,7 @@ import concourse.mybir as mybir
 FEATURES = 128
 NODES = 1024
 EDGES = 1024
-PIECE = 512
+PIECE = 256
 BLOCK = 32
 RUNS = EDGES // BLOCK
 CUTOFF = 5.0
@@ -20,25 +20,25 @@ def tile_edgefeatureinit_kernel(tc, table, w_src, w_dst, w_rbf, dist, w0, b0, b,
     nc = tc.nc
     with (
         tc.tile_pool(name="held", bufs=1) as held,
-        tc.tile_pool(name="work", bufs=2) as work,
+        tc.tile_pool(name="work", bufs=4) as work,
         tc.psum_pool(name="psum", bufs=1) as psum,
     ):
-        offsets = held.tile([FEATURES, 2 * EDGES // 16], U16, name="offsets")
-        nc.sync.dma_start(offsets[:], offs)
-        nodes = held.tile([FEATURES, NODES], BF16, name="nodes")
-        nc.scalar.dma_start(nodes[:], table)
-        src_weights = held.tile([FEATURES, FEATURES], BF16, name="src_weights")
-        nc.sync.dma_start(src_weights[:], w_src)
         runs = held.tile([FEATURES, BLOCK], F32, name="runs", align_bytes=64)
         for group in range(FEATURES // BLOCK):
             queue = nc.sync if group % 2 == 0 else nc.scalar
             queue.dma_start(runs[group * BLOCK : (group + 1) * BLOCK, :], dist.rearrange("o (k i) -> (o k) i", i=BLOCK))
+        nodes = held.tile([FEATURES, NODES], BF16, name="nodes")
+        nc.scalar.dma_start(nodes[:], table)
+        offsets = held.tile([FEATURES, 2 * EDGES // 16], U16, name="offsets")
+        nc.sync.dma_start(offsets[:], offs)
+        src_weights = held.tile([FEATURES, FEATURES], BF16, name="src_weights")
+        nc.sync.dma_start(src_weights[:], w_src)
         dst_weights = held.tile([FEATURES, FEATURES], BF16, name="dst_weights")
         nc.sync.dma_start(dst_weights[:], w_dst)
         w0_col = held.tile([FEATURES, 1], F32, name="w0_col")
-        nc.scalar.dma_start(w0_col[:], w0)
+        nc.sync.dma_start(w0_col[:], w0)
         b0_col = held.tile([FEATURES, 1], F32, name="b0_col")
-        nc.scalar.dma_start(b0_col[:], b0)
+        nc.sync.dma_start(b0_col[:], b0)
         rbf_weights = held.tile([FEATURES, FEATURES], BF16, name="rbf_weights")
         nc.sync.dma_start(rbf_weights[:], w_rbf)
         b_col = held.tile([FEATURES, 1], F32, name="b_col")

@@ -8,6 +8,7 @@ EDGES = 1024
 PIECE = 256
 BLOCK = 32
 RUNS = EDGES // BLOCK
+WARM_UP = 5
 CUTOFF = 5.0
 FLOPS = 2 * 3 * FEATURES * FEATURES * EDGES
 
@@ -23,6 +24,12 @@ def tile_edgefeatureinit_kernel(tc, table, w_src, w_dst, w_rbf, dist, w0, b0, b,
         tc.tile_pool(name="work", bufs=4) as work,
         tc.psum_pool(name="psum", bufs=1) as psum,
     ):
+        zeros = held.tile([FEATURES, 2 * PIECE], BF16, name="zeros")
+        nc.vector.memset(zeros[:], 0.0)
+        unused = psum.tile([FEATURES, 2 * PIECE], F32, name="unused")
+        for turn in range(WARM_UP):
+            nc.tensor.matmul(unused[:], zeros[:, :FEATURES], zeros[:], start=True, stop=True)
+
         runs = held.tile([FEATURES, BLOCK], F32, name="runs", align_bytes=64)
         for group in range(FEATURES // BLOCK):
             queue = nc.sync if group % 2 == 0 else nc.scalar

import math

import concourse.mybir as mybir

FEATURES = 128
NODES = 1024
EDGES = 1024
PIECE = 256
BLOCK = 32
RUNS = EDGES // BLOCK
WARM_UP = 5
CUTOFF = 5.0
FLOPS = 2 * 3 * FEATURES * FEATURES * EDGES

BF16, F32, I32, U16 = mybir.dt.bfloat16, mybir.dt.float32, mybir.dt.int32, mybir.dt.uint16
ACT = mybir.ActivationFunctionType
ALU = mybir.AluOpType


def tile_edgefeatureinit_kernel(tc, table, w_src, w_dst, w_rbf, dist, w0, b0, b, w1, offs, out):
    nc = tc.nc
    with (
        tc.tile_pool(name="held", bufs=1) as held,
        tc.tile_pool(name="work", bufs=4) as work,
        tc.psum_pool(name="psum", bufs=1) as psum,
    ):
        zeros = held.tile([FEATURES, 2 * PIECE], BF16, name="zeros")
        nc.vector.memset(zeros[:], 0.0)
        unused = psum.tile([FEATURES, 2 * PIECE], F32, name="unused")
        for turn in range(WARM_UP):
            nc.tensor.matmul(unused[:], zeros[:, :FEATURES], zeros[:], start=True, stop=True)

        runs = held.tile([FEATURES, BLOCK], F32, name="runs", align_bytes=64)
        for group in range(FEATURES // BLOCK):
            queue = nc.sync if group % 2 == 0 else nc.scalar
            queue.dma_start(runs[group * BLOCK : (group + 1) * BLOCK, :], dist.rearrange("o (k i) -> (o k) i", i=BLOCK))
        nodes = held.tile([FEATURES, NODES], BF16, name="nodes")
        nc.scalar.dma_start(nodes[:], table)
        offsets = held.tile([FEATURES, 2 * EDGES // 16], U16, name="offsets")
        nc.sync.dma_start(offsets[:], offs)
        src_weights = held.tile([FEATURES, FEATURES], BF16, name="src_weights")
        nc.sync.dma_start(src_weights[:], w_src)
        dst_weights = held.tile([FEATURES, FEATURES], BF16, name="dst_weights")
        nc.sync.dma_start(dst_weights[:], w_dst)
        w0_col = held.tile([FEATURES, 1], F32, name="w0_col")
        nc.sync.dma_start(w0_col[:], w0)
        b0_col = held.tile([FEATURES, 1], F32, name="b0_col")
        nc.sync.dma_start(b0_col[:], b0)
        rbf_weights = held.tile([FEATURES, FEATURES], BF16, name="rbf_weights")
        nc.sync.dma_start(rbf_weights[:], w_rbf)
        b_col = held.tile([FEATURES, 1], F32, name="b_col")
        nc.sync.dma_start(b_col[:], b)
        w1_col = held.tile([FEATURES, 1], F32, name="w1_col")
        nc.sync.dma_start(w1_col[:], w1)

        scratch = held.tile([FEATURES, 1], F32, name="scratch")
        nc.vector.memset(scratch[:], 0.0)
        nc.scalar.activation(scratch[:], scratch[:], ACT.Sin)

        lengths = held.tile([FEATURES, RUNS], F32, name="lengths", align_bytes=64)
        nc.vector.transpose(lengths[:], runs[:])

        turns = held.tile([FEATURES, RUNS], I32, name="turns")
        nc.vector.tensor_scalar(turns[:], lengths[:], 0.5 / CUTOFF, None, ALU.mult)
        part = held.tile([FEATURES, RUNS], F32, name="part")
        nc.vector.scalar_tensor_tensor(part[:], lengths[:], 0.5 / CUTOFF, turns[:], ALU.mult, ALU.subtract)
        minus_t = held.tile([FEATURES, RUNS], F32, name="minus_t")
        nc.vector.scalar_tensor_tensor(minus_t[:], part[:], 0.5, part[:], ALU.is_gt, ALU.subtract)
        sine = held.tile([FEATURES, RUNS], F32, name="sine")
        nc.scalar.activation(sine[:], minus_t[:], ACT.Sin, scale=-2.0 * math.pi)
        inverse = held.tile([FEATURES, RUNS], F32, name="inverse")
        nc.vector.reciprocal(inverse[:], lengths[:])

        for piece in range(EDGES // PIECE):
            edges = slice(piece * PIECE, (piece + 1) * PIECE)
            src_list = offsets[:, piece * (PIECE // 16) : (piece + 1) * (PIECE // 16)]
            dst_list = offsets[:, (EDGES + piece * PIECE) // 16 : (EDGES + (piece + 1) * PIECE) // 16]
            piece_runs = slice(piece * (PIECE // BLOCK), (piece + 1) * (PIECE // BLOCK))
            wide = [FEATURES, PIECE // BLOCK, BLOCK]

            repeated = work.tile(wide, F32, name="repeated", align_bytes=64)
            nc.vector.scalar_tensor_tensor(
                repeated[:],
                sine[:, piece_runs].unsqueeze(2).to_broadcast(wide),
                math.sqrt(2.0 / CUTOFF),
                inverse[:, piece_runs].unsqueeze(2).to_broadcast(wide),
                ALU.mult,
                ALU.mult,
            )
            rbf = work.tile([FEATURES, PIECE], F32, name="rbf", align_bytes=64)
            nc.vector.transpose(rbf[:], repeated[:].rearrange("p k i -> p (k i)"))

            pre = psum.tile([FEATURES, PIECE], F32, name=f"pre{piece}")
            nc.tensor.matmul(pre[:], src_weights[:], nodes[:].indirect(src_list), start=True, stop=False)
            nc.tensor.matmul(pre[:], dst_weights[:], nodes[:].indirect(dst_list), start=False, stop=False)
            rbf0 = work.tile([FEATURES, PIECE], BF16, name="rbf0")
            nc.scalar.activation(rbf0[:], rbf[:], ACT.Silu, bias=b0_col[:], scale=w0_col[:])
            nc.tensor.matmul(pre[:], rbf_weights[:], rbf0[:], start=False, stop=True)

            gated = work.tile([FEATURES, PIECE], F32, name="gated")
            nc.scalar.activation(gated[:], pre[:], ACT.Silu, bias=b_col[:])
            result = work.tile([FEATURES, PIECE], F32, name="result")
            nc.vector.scalar_tensor_tensor(result[:], gated[:], w1_col[:], rbf[:], ALU.mult, ALU.mult)
            nc.sync.dma_start(out[:, edges], result[:])
